import numpy as np
import ml_dtypes


def mxq(x, axis, fmt="e4m3"):
    dtype, down = {"e4m3": (ml_dtypes.float8_e4m3fn, 7), "e5m2": (ml_dtypes.float8_e5m2, 14)}[fmt]
    v = np.moveaxis(np.asarray(x, np.float32).astype(ml_dtypes.bfloat16).astype(np.float64), axis, -1)
    blocks = v.reshape(v.shape[:-1] + (-1, 32))
    amax = np.abs(blocks).max(-1, keepdims=True)
    byte = np.maximum(np.where(amax > 0, np.frexp(amax)[1] - 1 + 127, 0) - down, 1)
    scale = np.exp2(byte - 127.0)
    codes = (blocks / scale).astype(np.float32).astype(dtype).astype(np.float64)
    return np.moveaxis((codes * scale).reshape(v.shape), -1, axis)


WIDE = False


def mx_kscale(k):
    if not WIDE:
        return np.ones(k)
    levels = np.array([10, -10, 5, -5, 0])
    a = np.random.permutation(np.resize(levels, k // 512 * 4)).reshape(k // 512, 4)
    idx = np.arange(k)
    return np.exp2(a[idx // 512, idx % 128 // 32])


BF16 = ml_dtypes.bfloat16


def bf(x):
    return np.asarray(x, np.float32).astype(BF16)


def f64(x):
    return np.asarray(x).astype(np.float64)


B, D, DO, H, T, P = 1024, 1024, 1024, 256, 8, 2


def setup_inputs():
    s = mx_kscale(D)
    return {"transformed": bf(np.random.standard_normal((B, D)) * 1.8 * s),
            "coeff": bf(np.random.standard_normal(B) * 0.45),
            "task_mat": bf(np.random.standard_normal((D, D)) / np.sqrt(D) / s[:, None] * s[None, :]),
            "Wp": bf(np.random.standard_normal((DO, D)) / np.sqrt(D) / s[None, :])}


def reference(transformed, coeff, task_mat, Wp):
    x = f64(transformed)
    y = x + f64(coeff)[:, None] * (mxq(x, 1, "e4m3") @ mxq(f64(task_mat), 0, "e4m3"))
    return mxq(y, 1, "e4m3") @ mxq(f64(Wp), 1, "e4m3").T

@@ -1,0 +1,250 @@
+from contextlib import ExitStack
+
+import concourse.mybir as mybir
+from concourse.masks import make_identity
+
+F32 = mybir.dt.float32
+BF16 = mybir.dt.bfloat16
+U32 = mybir.dt.uint32
+U8 = mybir.dt.uint8
+FP8X4 = mybir.dt.float8_e4m3fn_x4
+MULT = mybir.AluOpType.mult
+ADD = mybir.AluOpType.add
+
+P = 128
+FLOPS = 2 * 2 * 1024 * 1024 * 1024
+VCOLS = 352
+
+ORDER = [
+    ("LT", 0, 0), ("LC",), ("LT", 0, 1), ("CT",), ("LX", 0),
+    ("CC",), ("LT", 1, 0), ("LT", 1, 1), ("RV", 0, 0), ("RS", 0, 0),
+    ("XT", 0), ("RS", 0, 1), ("LX", 1), ("RV", 0, 1), ("LX", 2),
+    ("XC", 0, "S"), ("QT", 0, 0), ("LX", 3), ("QT", 0, 1), ("LX", 4),
+    ("RS", 1, 0), ("XQ", 0), ("LX", 5), ("RV", 1, 0), ("XT", 1),
+    ("RS", 1, 1), ("LW", 0), ("S1", 0, 0, 0), ("QT", 1, 0), ("S1", 0, 1, 0),
+    ("XC", 1, "S"), ("XT", 2), ("RV", 1, 1), ("XT", 3), ("XC", 2, "S"),
+    ("XT", 4), ("QT", 1, 1), ("XT", 5), ("XC", 3, "S"), ("LX", 6),
+    ("S1", 0, 0, 1), ("XQ", 1), ("XC", 4, "S"), ("XQ", 2), ("S1", 0, 1, 1),
+    ("LX", 7), ("E", 0, 0), ("S1", 1, 0, 0), ("S1", 1, 0, 1), ("XC", 5, "S"),
+    ("LW", 1), ("S1", 1, 1, 0), ("E", 0, 1), ("S1", 1, 1, 1), ("S1", 2, 0, 0),
+    ("E", 1, 0), ("S1", 2, 0, 1), ("S1", 2, 1, 0), ("E", 1, 1), ("S1", 2, 1, 1),
+    ("WT", 0), ("E", 2, 0), ("YT", 0), ("WC", 0, "S"), ("E", 2, 1),
+    ("WT", 1), ("YT", 1), ("YC", 0, "S"), ("XQ", 3), ("XQ", 4),
+    ("WT", 2), ("XQ", 5), ("YT", 2), ("WC", 1, "V"), ("YC", 1, "S"),
+    ("WT", 3), ("YQ", 0), ("WT", 4), ("WC", 2, "V"), ("WT", 5),
+    ("YC", 2, "S"), ("WT", 6), ("YQ", 1), ("XT", 6), ("WC", 3, "V"),
+    ("WT", 7), ("XT", 7), ("WC", 4, "S"), ("WQ", 0, 0), ("S1", 3, 0, 0),
+    ("S1", 3, 0, 1), ("WQ", 0, 1), ("WC", 5, "S"), ("S1", 3, 1, 0), ("S1", 3, 1, 1),
+    ("YQ", 2), ("WC", 6, "S"), ("S1", 4, 0, 0), ("E", 3, 0), ("S2", 0, 0),
+    ("XC", 6, "S"), ("E", 3, 1), ("S2", 1, 0), ("WC", 7, "S"), ("XQ", 6),
+    ("S2", 2, 0), ("XC", 7, "V"), ("OC", 0, 0, "S"), ("S1", 4, 0, 1), ("WQ", 1, 0),
+    ("S1", 4, 1, 0), ("OC", 1, 0, "S"), ("ST", 0, 0), ("S1", 4, 1, 1), ("S1", 5, 0, 0),
+    ("WQ", 1, 1), ("OC", 2, 0, "S"), ("ST", 1, 0), ("S1", 5, 0, 1), ("S1", 5, 1, 0),
+    ("E", 4, 0), ("S1", 5, 1, 1), ("ST", 2, 0), ("S2", 0, 1), ("E", 4, 1),
+    ("S2", 1, 1), ("E", 5, 0), ("OC", 0, 1, "S"), ("S2", 2, 1), ("E", 5, 1),
+    ("OC", 1, 1, "S"), ("ST", 0, 1), ("S1", 6, 0, 0), ("XQ", 7), ("S1", 6, 0, 1),
+    ("OC", 2, 1, "S"), ("ST", 1, 1), ("S1", 6, 1, 0), ("E", 6, 0), ("S1", 6, 1, 1),
+    ("S1", 7, 0, 0), ("ST", 2, 1), ("S1", 7, 0, 1), ("E", 6, 1), ("S1", 7, 1, 0),
+    ("S1", 7, 1, 1), ("E", 7, 0), ("YT", 3), ("E", 7, 1), ("YT", 4),
+    ("YC", 3, "S"), ("YT", 5), ("YC", 4, "V"), ("YT", 6), ("YC", 5, "S"),
+    ("YT", 7), ("YQ", 3), ("YQ", 4), ("YC", 7, "V"), ("S2", 3, 0),
+    ("YC", 6, "S"), ("S2", 3, 1), ("YQ", 5), ("OC", 3, 0, "S"), ("S2", 4, 0),
+    ("YQ", 6), ("YQ", 7), ("OC", 3, 1, "S"), ("S2", 4, 1), ("ST", 3, 0),
+    ("OC", 4, 0, "V"), ("S2", 5, 0), ("ST", 3, 1), ("OC", 4, 1, "S"), ("S2", 5, 1),
+    ("ST", 4, 0), ("OC", 5, 0, "S"), ("S2", 6, 0), ("ST", 4, 1), ("OC", 5, 1, "V"),
+    ("S2", 6, 1), ("ST", 5, 0), ("OC", 6, 0, "S"), ("S2", 7, 0), ("ST", 5, 1),
+    ("OC", 6, 1, "S"), ("S2", 7, 1), ("ST", 6, 0), ("OC", 7, 0, "V"), ("ST", 6, 1),
+    ("OC", 7, 1, "S"), ("ST", 7, 0), ("ST", 7, 1),
+]
+
+
+def tile_precomputedmetanet_pb_kernel(tc, transformed, coeff, task_mat, Wp, out):
+    nc = tc.nc
+    with ExitStack() as ctx:
+        keep = ctx.enter_context(tc.tile_pool(name="keep", bufs=1))
+        psum = ctx.enter_context(tc.psum_pool(name="psum", bufs=8))
+        ctx.enter_context(tc.manual_schedule())
+
+        ident_b = keep.tile([P, P], BF16, name="ident_b")
+        ident_f = keep.tile([P, P], F32, name="ident_f")
+        crow = keep.tile([P, P], BF16, name="crow")
+        c_sb = keep.tile([P, 8], F32, name="c_sb")
+        nc.vector.memset(crow[:], 0.0)
+        make_identity(nc, ident_b[:])
+        make_identity(nc, ident_f[:])
+
+        traw = keep.tile([P, 2, 4, 1024], BF16, name="traw")
+        tcod = keep.tile([P, 2, 1024], U32, name="tcod", align_bytes=64)
+        tscl = keep.tile([P, 2, 1024], U8, name="tscl", align_bytes=64)
+        wraw = keep.tile([P, 8, 1024], BF16, name="wraw")
+        wcod = keep.tile([P, 2, 1024], U32, name="wcod", align_bytes=64)
+        wscl = keep.tile([P, 2, 1024], U8, name="wscl", align_bytes=64)
+        tgrp = {}
+        for g in range(2):
+            for c in range(2):
+                tgrp[(g, c)] = keep.tile([P, 512, 4], BF16, name="tgrp%d%d" % (g, c), align_bytes=64)
+        wgrp = [keep.tile([P, 2, 2048], BF16, name="wgrp%d" % c, align_bytes=64) for c in range(2)]
+        x_sb = [keep.tile([P, 1024], BF16, name="x_sb%d" % i) for i in range(8)]
+        xgrp = [keep.tile([P, 1024], BF16, name="xgrp%d" % i, align_bytes=64) for i in range(8)]
+        xcod = [keep.tile([P, 256], U32, name="xcod%d" % i, align_bytes=64) for i in range(8)]
+        xscl = [keep.tile([P, 256], U8, name="xscl%d" % i, align_bytes=64) for i in range(8)]
+        y_sb = [keep.tile([P, 2, 512], BF16, name="y_sb%d" % i) for i in range(8)]
+        ygrp = [keep.tile([P, 1024], BF16, name="ygrp%d" % i, align_bytes=64) for i in range(8)]
+        ycod = [keep.tile([P, 256], U32, name="ycod%d" % i, align_bytes=64) for i in range(8)]
+        yscl = [keep.tile([P, 256], U8, name="yscl%d" % i, align_bytes=64) for i in range(8)]
+        obuf = [keep.tile([P, 1024], F32, name="obuf%d" % i) for i in range(8)]
+        bank = {}
+
+        def copy(eng, dst, src):
+            if eng == "V":
+                nc.vector.tensor_copy(out=dst, in_=src)
+            else:
+                nc.scalar.copy(out=dst, in_=src)
+
+        def new_bank(key, shape, dtype):
+            t = psum.tile(shape, dtype, name="ps", tag="ps")
+            bank[key] = t
+            return t
+
+        def op_lc():
+            nc.scalar.dma_start(out=crow[0:8, :], in_=coeff.rearrange("(i p) -> i p", p=P))
+
+        def op_lt(g, u):
+            r0 = 512 * g + 256 * u
+            nc.sync.dma_start(
+                out=traw[:, g, 2 * u : 2 * u + 2, :],
+                in_=task_mat[r0 : r0 + 256, :].rearrange("(p e) d -> p e d", e=2),
+            )
+
+        def op_lx(i):
+            nc.sync.dma_start(out=x_sb[i][:], in_=transformed[P * i : P * i + P, :])
+
+        def op_lw(c):
+            nc.sync.dma_start(
+                out=wraw[:, 4 * c : 4 * c + 4, :],
+                in_=Wp[512 * c : 512 * c + 512, :].rearrange("(j p) d -> p j d", p=P),
+            )
+
+        def op_ct():
+            t = new_bank("c", [P, P], BF16)
+            nc.tensor.transpose(t[:], crow[:], ident_b[:])
+
+        def op_cc():
+            nc.vector.tensor_copy(out=c_sb[:], in_=bank["c"][:, 0:8])
+
+        def regroup(eng, g, c, lo, hi):
+            src = traw[:, g, :, 512 * c + lo : 512 * c + hi].rearrange("p t (c i) -> p c t i", i=4)
+            dst = tgrp[(g, c)][:, lo:hi, :].rearrange("p (c i) t -> p c t i", i=4)
+            copy(eng, dst, src)
+
+        def op_rv(g, c):
+            regroup("V", g, c, 0, VCOLS)
+
+        def op_rs(g, c):
+            regroup("S", g, c, VCOLS, 512)
+
+        def op_qt(g, c):
+            nc.vector.quantize_mx(
+                out=tcod[:, g, 512 * c : 512 * c + 512].bitcast(FP8X4),
+                scales=tscl[:, g, 512 * c : 512 * c + 512],
+                in_=tgrp[(g, c)][:].rearrange("p d t -> p (d t)"),
+            )
+
+        def word_transposes(key, rows):
+            t = new_bank(key, [P, 4, P], F32)
+            words = rows.bitcast(F32)
+            for q in range(4):
+                nc.tensor.transpose(t[:, q, :], words[:, P * q : P * q + P], ident_f[:])
+
+        def op_xt(i):
+            word_transposes(("x", i), x_sb[i][:])
+
+        def op_xc(i, eng):
+            dst = xgrp[i][:].bitcast(F32).rearrange("p (g b u) -> p g b u", g=2, b=P, u=2)
+            copy(eng, dst, bank[("x", i)][:].rearrange("p (g u) b -> p g b u", g=2, u=2))
+
+        def op_xq(i):
+            nc.vector.quantize_mx(out=xcod[i][:].bitcast(FP8X4), scales=xscl[i][:], in_=xgrp[i][:])
+
+        def op_s1(i, c, g):
+            if g == 0:
+                new_bank(("z", i, c), [P, 512], F32)
+            nc.tensor.matmul_mx(
+                out=bank[("z", i, c)][:],
+                lhsT=xcod[i][:, P * g : P * g + P].bitcast(FP8X4),
+                lhsT_scale=xscl[i][:, P * g : P * g + P],
+                rhs=tcod[:, g, 512 * c : 512 * c + 512].bitcast(FP8X4),
+                rhs_scale=tscl[:, g, 512 * c : 512 * c + 512],
+                start=(g == 0),
+                stop=(g == 1),
+            )
+
+        def op_e(i, c):
+            nc.vector.scalar_tensor_tensor(
+                out=y_sb[i][:, :, 256 * c : 256 * c + 256],
+                in0=bank[("z", i, c)][:].rearrange("p (w e) -> p e w", e=2),
+                scalar=c_sb[:, i : i + 1],
+                in1=x_sb[i][:, 512 * c : 512 * c + 512].rearrange("p (w e) -> p e w", e=2),
+                op0=MULT,
+                op1=ADD,
+            )
+
+        def op_yt(i):
+            t = new_bank(("y", i), [P, 8, P], BF16)
+            for g in range(2):
+                for u in range(2):
+                    for e in range(2):
+                        q = 2 * g + u
+                        nc.tensor.transpose(t[:, 4 * g + 2 * u + e, :], y_sb[i][:, e, P * q : P * q + P], ident_b[:])
+
+        def op_yc(i, eng):
+            dst = ygrp[i][:].rearrange("p (g b t) -> p g b t", g=2, b=P, t=4)
+            copy(eng, dst, bank[("y", i)][:].rearrange("p (g t) b -> p g b t", g=2, t=4))
+
+        def op_yq(i):
+            nc.vector.quantize_mx(out=ycod[i][:].bitcast(FP8X4), scales=yscl[i][:], in_=ygrp[i][:])
+
+        def op_wt(j):
+            word_transposes(("w", j), wraw[:, j, :])
+
+        def op_wc(j, eng):
+            lo = P * (j % 4)
+            dst = wgrp[j // 4][:].bitcast(F32).rearrange("p g (o u) -> p g o u", u=2)[:, :, lo : lo + P, :]
+            copy(eng, dst, bank[("w", j)][:].rearrange("p (g u) o -> p g o u", g=2, u=2))
+
+        def op_wq(c, g):
+            nc.vector.quantize_mx(
+                out=wcod[:, g, 512 * c : 512 * c + 512].bitcast(FP8X4),
+                scales=wscl[:, g, 512 * c : 512 * c + 512],
+                in_=wgrp[c][:, g, :],
+            )
+
+        def op_s2(i, c):
+            t = new_bank(("o", i, c), [P, 512], F32)
+            for g in range(2):
+                nc.tensor.matmul_mx(
+                    out=t[:],
+                    lhsT=ycod[i][:, P * g : P * g + P].bitcast(FP8X4),
+                    lhsT_scale=yscl[i][:, P * g : P * g + P],
+                    rhs=wcod[:, g, 512 * c : 512 * c + 512].bitcast(FP8X4),
+                    rhs_scale=wscl[:, g, 512 * c : 512 * c + 512],
+                    start=(g == 0),
+                    stop=(g == 1),
+                )
+
+        def op_oc(i, c, eng):
+            copy(eng, obuf[i][:, 512 * c : 512 * c + 512], bank[("o", i, c)][:])
+
+        def op_st(i, c):
+            nc.sync.dma_start(
+                out=out[P * i : P * i + P, 512 * c : 512 * c + 512], in_=obuf[i][:, 512 * c : 512 * c + 512]
+            )
+
+        ops = {
+            "LC": op_lc, "LT": op_lt, "LX": op_lx, "LW": op_lw, "CT": op_ct, "CC": op_cc,
+            "RV": op_rv, "RS": op_rs, "QT": op_qt, "XT": op_xt, "XC": op_xc, "XQ": op_xq,
+            "S1": op_s1, "E": op_e, "YT": op_yt, "YC": op_yc, "YQ": op_yq,
+            "WT": op_wt, "WC": op_wc, "WQ": op_wq, "S2": op_s2, "OC": op_oc, "ST": op_st,
+        }
+        for step in ORDER:
+            ops[step[0]](*step[1:])

@@ -16,45 +16,42 @@ FLOPS = 2 * 2 * 1024 * 1024 * 1024
 VCOLS = 352
 
 ORDER = [
-    ("LT", 0, 0), ("LC",), ("LT", 0, 1), ("CT",), ("LX", 0),
-    ("CC",), ("LT", 1, 0), ("LT", 1, 1), ("RV", 0, 0), ("RS", 0, 0),
-    ("XT", 0), ("RS", 0, 1), ("LX", 1), ("RV", 0, 1), ("LX", 2),
-    ("XC", 0, "S"), ("QT", 0, 0), ("LX", 3), ("QT", 0, 1), ("LX", 4),
-    ("RS", 1, 0), ("XQ", 0), ("LX", 5), ("RV", 1, 0), ("XT", 1),
-    ("RS", 1, 1), ("LW", 0), ("S1", 0, 0, 0), ("QT", 1, 0), ("S1", 0, 1, 0),
-    ("XC", 1, "S"), ("XT", 2), ("RV", 1, 1), ("XT", 3), ("XC", 2, "S"),
-    ("XT", 4), ("QT", 1, 1), ("XT", 5), ("XC", 3, "S"), ("LX", 6),
-    ("S1", 0, 0, 1), ("XQ", 1), ("XC", 4, "S"), ("XQ", 2), ("S1", 0, 1, 1),
-    ("LX", 7), ("E", 0, 0), ("S1", 1, 0, 0), ("S1", 1, 0, 1), ("XC", 5, "S"),
-    ("LW", 1), ("S1", 1, 1, 0), ("E", 0, 1), ("S1", 1, 1, 1), ("S1", 2, 0, 0),
-    ("E", 1, 0), ("S1", 2, 0, 1), ("S1", 2, 1, 0), ("E", 1, 1), ("S1", 2, 1, 1),
-    ("WT", 0), ("E", 2, 0), ("YT", 0), ("WC", 0, "S"), ("E", 2, 1),
-    ("WT", 1), ("YT", 1), ("YC", 0, "S"), ("XQ", 3), ("XQ", 4),
-    ("WT", 2), ("XQ", 5), ("YT", 2), ("WC", 1, "V"), ("YC", 1, "S"),
-    ("WT", 3), ("YQ", 0), ("WT", 4), ("WC", 2, "V"), ("WT", 5),
-    ("YC", 2, "S"), ("WT", 6), ("YQ", 1), ("XT", 6), ("WC", 3, "V"),
-    ("WT", 7), ("XT", 7), ("WC", 4, "S"), ("WQ", 0, 0), ("S1", 3, 0, 0),
-    ("S1", 3, 0, 1), ("WQ", 0, 1), ("WC", 5, "S"), ("S1", 3, 1, 0), ("S1", 3, 1, 1),
-    ("YQ", 2), ("WC", 6, "S"), ("S1", 4, 0, 0), ("E", 3, 0), ("S2", 0, 0),
-    ("XC", 6, "S"), ("E", 3, 1), ("S2", 1, 0), ("WC", 7, "S"), ("XQ", 6),
-    ("S2", 2, 0), ("XC", 7, "V"), ("OC", 0, 0, "S"), ("S1", 4, 0, 1), ("WQ", 1, 0),
-    ("S1", 4, 1, 0), ("OC", 1, 0, "S"), ("ST", 0, 0), ("S1", 4, 1, 1), ("S1", 5, 0, 0),
-    ("WQ", 1, 1), ("OC", 2, 0, "S"), ("ST", 1, 0), ("S1", 5, 0, 1), ("S1", 5, 1, 0),
-    ("E", 4, 0), ("S1", 5, 1, 1), ("ST", 2, 0), ("S2", 0, 1), ("E", 4, 1),
-    ("S2", 1, 1), ("E", 5, 0), ("OC", 0, 1, "S"), ("S2", 2, 1), ("E", 5, 1),
-    ("OC", 1, 1, "S"), ("ST", 0, 1), ("S1", 6, 0, 0), ("XQ", 7), ("S1", 6, 0, 1),
-    ("OC", 2, 1, "S"), ("ST", 1, 1), ("S1", 6, 1, 0), ("E", 6, 0), ("S1", 6, 1, 1),
-    ("S1", 7, 0, 0), ("ST", 2, 1), ("S1", 7, 0, 1), ("E", 6, 1), ("S1", 7, 1, 0),
-    ("S1", 7, 1, 1), ("E", 7, 0), ("YT", 3), ("E", 7, 1), ("YT", 4),
-    ("YC", 3, "S"), ("YT", 5), ("YC", 4, "V"), ("YT", 6), ("YC", 5, "S"),
-    ("YT", 7), ("YQ", 3), ("YQ", 4), ("YC", 7, "V"), ("S2", 3, 0),
-    ("YC", 6, "S"), ("S2", 3, 1), ("YQ", 5), ("OC", 3, 0, "S"), ("S2", 4, 0),
-    ("YQ", 6), ("YQ", 7), ("OC", 3, 1, "S"), ("S2", 4, 1), ("ST", 3, 0),
-    ("OC", 4, 0, "V"), ("S2", 5, 0), ("ST", 3, 1), ("OC", 4, 1, "S"), ("S2", 5, 1),
-    ("ST", 4, 0), ("OC", 5, 0, "S"), ("S2", 6, 0), ("ST", 4, 1), ("OC", 5, 1, "V"),
-    ("S2", 6, 1), ("ST", 5, 0), ("OC", 6, 0, "S"), ("S2", 7, 0), ("ST", 5, 1),
-    ("OC", 6, 1, "S"), ("S2", 7, 1), ("ST", 6, 0), ("OC", 7, 0, "V"), ("ST", 6, 1),
-    ("OC", 7, 1, "S"), ("ST", 7, 0), ("ST", 7, 1),
+    ("LT", 0, 0), ("LC",), ("LT", 0, 1), ("CC",), ("LX", 0),
+    ("LT", 1, 0), ("RV", 0, 0), ("RS", 0, 0), ("LT", 1, 1), ("RS", 0, 1),
+    ("RV", 0, 1), ("XT", 0), ("LX", 1), ("XT", 1), ("QT", 0, 0),
+    ("XC", 0, "S"), ("QT", 0, 1), ("XC", 1, "S"), ("LX", 2), ("XQ", 0),
+    ("XQ", 1), ("RS", 1, 0), ("RV", 1, 0), ("S1", 0, 0, 0), ("LW", 0),
+    ("S1", 0, 1, 0), ("S1", 1, 0, 0), ("RS", 1, 1), ("RV", 1, 1), ("S1", 1, 1, 0),
+    ("XT", 2), ("QT", 1, 0), ("XT", 3), ("XC", 2, "S"), ("XT", 4),
+    ("QT", 1, 1), ("XC", 3, "S"), ("XT", 5), ("LX", 3), ("XQ", 2),
+    ("S1", 0, 0, 1), ("XC", 5, "V"), ("XC", 4, "S"), ("S1", 0, 1, 1), ("S1", 1, 0, 1),
+    ("E", 0, 0), ("S1", 1, 1, 1), ("LW", 1), ("S1", 2, 0, 0), ("E", 0, 1),
+    ("S1", 2, 0, 1), ("S1", 2, 1, 0), ("S1", 2, 1, 1), ("E", 1, 0), ("WT", 0),
+    ("E", 1, 1), ("YT", 0), ("WC", 0, "S"), ("WT", 1), ("E", 2, 0),
+    ("YT", 1), ("YC", 0, "S"), ("E", 2, 1), ("WT", 2), ("WT", 3),
+    ("XQ", 3), ("WC", 1, "S"), ("YT", 2), ("XQ", 4), ("YQ", 0),
+    ("XT", 6), ("YC", 1, "S"), ("XQ", 5), ("WT", 4), ("WC", 2, "V"),
+    ("WT", 5), ("WT", 6), ("YC", 2, "V"), ("WC", 3, "S"), ("WT", 7),
+    ("XT", 7), ("WC", 4, "S"), ("S1", 3, 0, 0), ("WQ", 0, 0), ("S1", 3, 0, 1),
+    ("WC", 5, "S"), ("S1", 3, 1, 0), ("WQ", 0, 1), ("S1", 3, 1, 1), ("WC", 6, "S"),
+    ("S1", 4, 0, 0), ("YQ", 1), ("S1", 4, 0, 1), ("YQ", 2), ("XC", 6, "S"),
+    ("S2", 0, 0), ("E", 3, 0), ("WC", 7, "S"), ("S2", 1, 0), ("E", 3, 1),
+    ("S2", 2, 0), ("OC", 0, 0, "S"), ("WQ", 1, 0), ("S1", 4, 1, 0), ("OC", 1, 0, "S"),
+    ("S1", 4, 1, 1), ("WQ", 1, 1), ("S1", 5, 0, 0), ("OC", 2, 0, "S"), ("S1", 5, 0, 1),
+    ("E", 4, 0), ("S1", 5, 1, 0), ("XC", 7, "S"), ("S2", 0, 1), ("E", 4, 1),
+    ("S2", 1, 1), ("E", 5, 0), ("OC", 0, 1, "S"), ("S2", 2, 1), ("XQ", 6),
+    ("OC", 1, 1, "S"), ("ST", 0), ("XQ", 7), ("S1", 5, 1, 1), ("OC", 2, 1, "V"),
+    ("S1", 6, 0, 0), ("S1", 6, 0, 1), ("S1", 6, 1, 0), ("E", 5, 1), ("ST", 1),
+    ("S1", 6, 1, 1), ("S1", 7, 0, 0), ("E", 6, 0), ("S1", 7, 0, 1), ("S1", 7, 1, 0),
+    ("E", 6, 1), ("ST", 2), ("S1", 7, 1, 1), ("YT", 3), ("E", 7, 0),
+    ("YT", 4), ("E", 7, 1), ("YC", 3, "S"), ("YT", 5), ("YC", 4, "V"),
+    ("YT", 6), ("YC", 5, "S"), ("YT", 7), ("YQ", 3), ("YQ", 4),
+    ("YC", 6, "S"), ("YC", 7, "V"), ("S2", 3, 0), ("S2", 3, 1), ("OC", 3, 0, "S"),
+    ("YQ", 5), ("S2", 4, 0), ("YQ", 6), ("YQ", 7), ("OC", 3, 1, "S"),
+    ("S2", 4, 1), ("OC", 4, 0, "V"), ("S2", 5, 0), ("ST", 3), ("OC", 4, 1, "S"),
+    ("S2", 5, 1), ("OC", 5, 0, "S"), ("S2", 6, 0), ("ST", 4), ("OC", 5, 1, "V"),
+    ("S2", 6, 1), ("OC", 6, 0, "S"), ("S2", 7, 0), ("ST", 5), ("OC", 6, 1, "S"),
+    ("S2", 7, 1), ("OC", 7, 0, "V"), ("OC", 7, 1, "S"), ("ST", 6), ("ST", 7),
 ]
 
 
@@ -67,9 +64,8 @@ def tile_precomputedmetanet_pb_kernel(tc, transformed, coeff, task_mat, Wp, out)
 
         ident_b = keep.tile([P, P], BF16, name="ident_b")
         ident_f = keep.tile([P, P], F32, name="ident_f")
-        crow = keep.tile([P, P], BF16, name="crow")
+        c_bf = keep.tile([P, 8], BF16, name="c_bf")
         c_sb = keep.tile([P, 8], F32, name="c_sb")
-        nc.vector.memset(crow[:], 0.0)
         make_identity(nc, ident_b[:])
         make_identity(nc, ident_f[:])
 
@@ -84,7 +80,10 @@ def tile_precomputedmetanet_pb_kernel(tc, transformed, coeff, task_mat, Wp, out)
             for c in range(2):
                 tgrp[(g, c)] = keep.tile([P, 512, 4], BF16, name="tgrp%d%d" % (g, c), align_bytes=64)
         wgrp = [keep.tile([P, 2, 2048], BF16, name="wgrp%d" % c, align_bytes=64) for c in range(2)]
-        x_sb = [keep.tile([P, 1024], BF16, name="x_sb%d" % i) for i in range(8)]
+        x_all = keep.tile([P, 8, 1024], BF16, name="x_all")
+        x_sb = [x_all[:, i, :] for i in range(8)]
+        x_dram = transformed.rearrange("(p i) d -> p i d", i=8)
+        out_dram = out.rearrange("(p i) o -> p i o", i=8)
         xgrp = [keep.tile([P, 1024], BF16, name="xgrp%d" % i, align_bytes=64) for i in range(8)]
         xcod = [keep.tile([P, 256], U32, name="xcod%d" % i, align_bytes=64) for i in range(8)]
         xscl = [keep.tile([P, 256], U8, name="xscl%d" % i, align_bytes=64) for i in range(8)]
@@ -107,7 +106,7 @@ def tile_precomputedmetanet_pb_kernel(tc, transformed, coeff, task_mat, Wp, out)
             return t
 
         def op_lc():
-            nc.scalar.dma_start(out=crow[0:8, :], in_=coeff.rearrange("(i p) -> i p", p=P))
+            nc.scalar.dma_start(out=c_bf[:], in_=coeff.rearrange("(p i) -> p i", i=8))
 
         def op_lt(g, u):
             r0 = 512 * g + 256 * u
@@ -116,8 +115,8 @@ def tile_precomputedmetanet_pb_kernel(tc, transformed, coeff, task_mat, Wp, out)
                 in_=task_mat[r0 : r0 + 256, :].rearrange("(p e) d -> p e d", e=2),
             )
 
-        def op_lx(i):
-            nc.sync.dma_start(out=x_sb[i][:], in_=transformed[P * i : P * i + P, :])
+        def op_lx(a):
+            nc.sync.dma_start(out=x_all[:, 2 * a : 2 * a + 2, :], in_=x_dram[:, 2 * a : 2 * a + 2, :])
 
         def op_lw(c):
             nc.sync.dma_start(
@@ -125,12 +124,8 @@ def tile_precomputedmetanet_pb_kernel(tc, transformed, coeff, task_mat, Wp, out)
                 in_=Wp[512 * c : 512 * c + 512, :].rearrange("(j p) d -> p j d", p=P),
             )
 
-        def op_ct():
-            t = new_bank("c", [P, P], BF16)
-            nc.tensor.transpose(t[:], crow[:], ident_b[:])
-
         def op_cc():
-            nc.vector.tensor_copy(out=c_sb[:], in_=bank["c"][:, 0:8])
+            nc.vector.tensor_copy(out=c_sb[:], in_=c_bf[:])
 
         def regroup(eng, g, c, lo, hi):
             src = traw[:, g, :, 512 * c + lo : 512 * c + hi].rearrange("p t (c i) -> p c t i", i=4)
@@ -235,13 +230,11 @@ def tile_precomputedmetanet_pb_kernel(tc, transformed, coeff, task_mat, Wp, out)
         def op_oc(i, c, eng):
             copy(eng, obuf[i][:, 512 * c : 512 * c + 512], bank[("o", i, c)][:])
 
-        def op_st(i, c):
-            nc.sync.dma_start(
-                out=out[P * i : P * i + P, 512 * c : 512 * c + 512], in_=obuf[i][:, 512 * c : 512 * c + 512]
-            )
+        def op_st(i):
+            nc.sync.dma_start(out=out_dram[:, i, :], in_=obuf[i][:])
 
         ops = {
-            "LC": op_lc, "LT": op_lt, "LX": op_lx, "LW": op_lw, "CT": op_ct, "CC": op_cc,
+            "LC": op_lc, "LT": op_lt, "LX": op_lx, "LW": op_lw, "CC": op_cc,
             "RV": op_rv, "RS": op_rs, "QT": op_qt, "XT": op_xt, "XC": op_xc, "XQ": op_xq,
             "S1": op_s1, "E": op_e, "YT": op_yt, "YC": op_yc, "YQ": op_yq,
             "WT": op_wt, "WC": op_wc, "WQ": op_wq, "S2": op_s2, "OC": op_oc, "ST": op_st,

@@ -19,39 +19,39 @@ ORDER = [
     ("LT", 0, 0), ("LC",), ("LT", 0, 1), ("CC",), ("LX", 0),
     ("LT", 1, 0), ("RV", 0, 0), ("RS", 0, 0), ("LT", 1, 1), ("RS", 0, 1),
     ("RV", 0, 1), ("XT", 0), ("LX", 1), ("XT", 1), ("QT", 0, 0),
-    ("XC", 0, "S"), ("QT", 0, 1), ("XC", 1, "S"), ("LX", 2), ("XQ", 0),
-    ("XQ", 1), ("RS", 1, 0), ("RV", 1, 0), ("S1", 0, 0, 0), ("LW", 0),
-    ("S1", 0, 1, 0), ("S1", 1, 0, 0), ("RS", 1, 1), ("RV", 1, 1), ("S1", 1, 1, 0),
-    ("XT", 2), ("QT", 1, 0), ("XT", 3), ("XC", 2, "S"), ("XT", 4),
-    ("QT", 1, 1), ("XC", 3, "S"), ("XT", 5), ("LX", 3), ("XQ", 2),
-    ("S1", 0, 0, 1), ("XC", 5, "V"), ("XC", 4, "S"), ("S1", 0, 1, 1), ("S1", 1, 0, 1),
-    ("E", 0, 0), ("S1", 1, 1, 1), ("LW", 1), ("S1", 2, 0, 0), ("E", 0, 1),
-    ("S1", 2, 0, 1), ("S1", 2, 1, 0), ("S1", 2, 1, 1), ("E", 1, 0), ("WT", 0),
-    ("E", 1, 1), ("YT", 0), ("WC", 0, "S"), ("WT", 1), ("E", 2, 0),
-    ("YT", 1), ("YC", 0, "S"), ("E", 2, 1), ("WT", 2), ("WT", 3),
-    ("XQ", 3), ("WC", 1, "S"), ("YT", 2), ("XQ", 4), ("YQ", 0),
-    ("XT", 6), ("YC", 1, "S"), ("XQ", 5), ("WT", 4), ("WC", 2, "V"),
-    ("WT", 5), ("WT", 6), ("YC", 2, "V"), ("WC", 3, "S"), ("WT", 7),
-    ("XT", 7), ("WC", 4, "S"), ("S1", 3, 0, 0), ("WQ", 0, 0), ("S1", 3, 0, 1),
-    ("WC", 5, "S"), ("S1", 3, 1, 0), ("WQ", 0, 1), ("S1", 3, 1, 1), ("WC", 6, "S"),
-    ("S1", 4, 0, 0), ("YQ", 1), ("S1", 4, 0, 1), ("YQ", 2), ("XC", 6, "S"),
-    ("S2", 0, 0), ("E", 3, 0), ("WC", 7, "S"), ("S2", 1, 0), ("E", 3, 1),
-    ("S2", 2, 0), ("OC", 0, 0, "S"), ("WQ", 1, 0), ("S1", 4, 1, 0), ("OC", 1, 0, "S"),
-    ("S1", 4, 1, 1), ("WQ", 1, 1), ("S1", 5, 0, 0), ("OC", 2, 0, "S"), ("S1", 5, 0, 1),
-    ("E", 4, 0), ("S1", 5, 1, 0), ("XC", 7, "S"), ("S2", 0, 1), ("E", 4, 1),
-    ("S2", 1, 1), ("E", 5, 0), ("OC", 0, 1, "S"), ("S2", 2, 1), ("XQ", 6),
-    ("OC", 1, 1, "S"), ("ST", 0), ("XQ", 7), ("S1", 5, 1, 1), ("OC", 2, 1, "V"),
-    ("S1", 6, 0, 0), ("S1", 6, 0, 1), ("S1", 6, 1, 0), ("E", 5, 1), ("ST", 1),
-    ("S1", 6, 1, 1), ("S1", 7, 0, 0), ("E", 6, 0), ("S1", 7, 0, 1), ("S1", 7, 1, 0),
-    ("E", 6, 1), ("ST", 2), ("S1", 7, 1, 1), ("YT", 3), ("E", 7, 0),
-    ("YT", 4), ("E", 7, 1), ("YC", 3, "S"), ("YT", 5), ("YC", 4, "V"),
-    ("YT", 6), ("YC", 5, "S"), ("YT", 7), ("YQ", 3), ("YQ", 4),
-    ("YC", 6, "S"), ("YC", 7, "V"), ("S2", 3, 0), ("S2", 3, 1), ("OC", 3, 0, "S"),
-    ("YQ", 5), ("S2", 4, 0), ("YQ", 6), ("YQ", 7), ("OC", 3, 1, "S"),
-    ("S2", 4, 1), ("OC", 4, 0, "V"), ("S2", 5, 0), ("ST", 3), ("OC", 4, 1, "S"),
-    ("S2", 5, 1), ("OC", 5, 0, "S"), ("S2", 6, 0), ("ST", 4), ("OC", 5, 1, "V"),
-    ("S2", 6, 1), ("OC", 6, 0, "S"), ("S2", 7, 0), ("ST", 5), ("OC", 6, 1, "S"),
-    ("S2", 7, 1), ("OC", 7, 0, "V"), ("OC", 7, 1, "S"), ("ST", 6), ("ST", 7),
+    ("XC", 0, "S"), ("QT", 0, 1), ("XC", 1, "S"), ("LW", 0), ("XQ", 0),
+    ("XQ", 1), ("RS", 1, 0), ("RV", 1, 0), ("RS", 1, 1), ("RV", 1, 1),
+    ("XT", 2), ("S1", 0, 0, 0), ("LX", 2), ("XC", 2, "S"), ("QT", 1, 0),
+    ("QT", 1, 1), ("S1", 0, 0, 1), ("LX", 3), ("XQ", 2), ("S1", 0, 1, 0),
+    ("E", 0, 0), ("S1", 0, 1, 1), ("XT", 3), ("E", 0, 1), ("LW", 1),
+    ("WT", 0), ("XC", 3, "S"), ("WT", 1), ("WC", 0, "V"), ("S1", 1, 0, 0),
+    ("WC", 1, "S"), ("S1", 1, 0, 1), ("XQ", 3), ("S1", 1, 1, 0), ("E", 1, 0),
+    ("S1", 1, 1, 1), ("XT", 4), ("E", 1, 1), ("YT", 0), ("XC", 4, "S"),
+    ("WT", 2), ("YC", 0, "V"), ("WT", 3), ("WC", 2, "S"), ("S1", 2, 0, 0),
+    ("S1", 2, 0, 1), ("WC", 3, "S"), ("S1", 2, 1, 0), ("YQ", 0), ("S1", 2, 1, 1),
+    ("E", 2, 0), ("XT", 5), ("WQ", 0, 0), ("YT", 1), ("XC", 5, "S"),
+    ("WT", 4), ("WQ", 0, 1), ("WT", 5), ("YC", 1, "S"), ("E", 2, 1),
+    ("S1", 3, 0, 0), ("S1", 3, 0, 1), ("XQ", 4), ("S1", 3, 1, 0), ("WC", 4, "S"),
+    ("XQ", 5), ("S1", 3, 1, 1), ("YQ", 1), ("XT", 6), ("WC", 5, "S"),
+    ("E", 3, 0), ("YT", 2), ("XC", 6, "S"), ("E", 3, 1), ("WT", 6),
+    ("WT", 7), ("YC", 2, "S"), ("XQ", 6), ("S1", 4, 0, 0), ("WC", 6, "V"),
+    ("S1", 4, 0, 1), ("S1", 4, 1, 0), ("E", 4, 0), ("S1", 4, 1, 1), ("WC", 7, "S"),
+    ("XT", 7), ("YQ", 2), ("YT", 3), ("WQ", 1, 0), ("XC", 7, "S"),
+    ("S1", 5, 0, 0), ("WQ", 1, 1), ("YC", 3, "S"), ("S1", 5, 0, 1), ("S1", 5, 1, 0),
+    ("E", 4, 1), ("S1", 5, 1, 1), ("S2", 0, 0), ("E", 5, 0), ("S2", 0, 1),
+    ("OC", 0, 0, "S"), ("YQ", 3), ("YT", 4), ("E", 5, 1), ("OC", 0, 1, "S"),
+    ("XQ", 7), ("S1", 6, 0, 0), ("YC", 4, "S"), ("S1", 6, 0, 1), ("ST", 0),
+    ("S1", 6, 1, 0), ("E", 6, 0), ("S1", 6, 1, 1), ("S2", 1, 0), ("E", 6, 1),
+    ("S2", 1, 1), ("OC", 1, 0, "S"), ("YQ", 4), ("YT", 5), ("OC", 1, 1, "S"),
+    ("S1", 7, 0, 0), ("YC", 5, "S"), ("S1", 7, 0, 1), ("ST", 1), ("S1", 7, 1, 0),
+    ("E", 7, 0), ("S1", 7, 1, 1), ("S2", 2, 0), ("E", 7, 1), ("S2", 2, 1),
+    ("OC", 2, 0, "S"), ("YQ", 5), ("YT", 6), ("OC", 2, 1, "S"), ("S2", 3, 0),
+    ("YC", 6, "S"), ("ST", 2), ("S2", 3, 1), ("OC", 3, 0, "V"), ("YT", 7),
+    ("OC", 3, 1, "S"), ("YQ", 6), ("S2", 4, 0), ("YC", 7, "S"), ("ST", 3),
+    ("S2", 4, 1), ("OC", 4, 0, "V"), ("S2", 5, 0), ("OC", 4, 1, "S"), ("YQ", 7),
+    ("S2", 5, 1), ("OC", 5, 0, "S"), ("ST", 4), ("S2", 6, 0), ("OC", 5, 1, "V"),
+    ("S2", 6, 1), ("OC", 6, 0, "S"), ("ST", 5), ("S2", 7, 0), ("OC", 6, 1, "S"),
+    ("S2", 7, 1), ("OC", 7, 0, "V"), ("ST", 6), ("OC", 7, 1, "S"), ("ST", 7),
 ]
 
 

@@ -12,47 +12,15 @@ MULT = mybir.AluOpType.mult
 ADD = mybir.AluOpType.add
 
 P = 128
-FLOPS = 2 * 2 * 1024 * 1024 * 1024
-VCOLS = 352
+SIZE = 1024
+TILES = SIZE // P
+HALF = 512
+PACK = 4
+FIRST = (0, 1, 2)
+REST = (3, 4, 5, 6, 7)
+VECTOR_COLUMNS = 352
 
-ORDER = [
-    ("LT", 0, 0), ("LC",), ("LT", 0, 1), ("CC",), ("LX", 0),
-    ("LT", 1, 0), ("RV", 0, 0), ("RS", 0, 0), ("LT", 1, 1), ("RS", 0, 1),
-    ("RV", 0, 1), ("XT", 0), ("LX", 1), ("XT", 1), ("QT", 0, 0),
-    ("XC", 0, "S"), ("QT", 0, 1), ("XC", 1, "S"), ("LW", 0), ("XQ", 0),
-    ("XQ", 1), ("RS", 1, 0), ("RV", 1, 0), ("RS", 1, 1), ("RV", 1, 1),
-    ("XT", 2), ("S1", 0, 0, 0), ("LX", 2), ("XC", 2, "S"), ("QT", 1, 0),
-    ("QT", 1, 1), ("S1", 0, 0, 1), ("LX", 3), ("XQ", 2), ("S1", 0, 1, 0),
-    ("E", 0, 0), ("S1", 0, 1, 1), ("XT", 3), ("E", 0, 1), ("LW", 1),
-    ("WT", 0), ("XC", 3, "S"), ("WT", 1), ("WC", 0, "V"), ("S1", 1, 0, 0),
-    ("WC", 1, "S"), ("S1", 1, 0, 1), ("XQ", 3), ("S1", 1, 1, 0), ("E", 1, 0),
-    ("S1", 1, 1, 1), ("XT", 4), ("E", 1, 1), ("YT", 0), ("XC", 4, "S"),
-    ("WT", 2), ("YC", 0, "V"), ("WT", 3), ("WC", 2, "S"), ("S1", 2, 0, 0),
-    ("S1", 2, 0, 1), ("WC", 3, "S"), ("S1", 2, 1, 0), ("YQ", 0), ("S1", 2, 1, 1),
-    ("E", 2, 0), ("XT", 5), ("WQ", 0, 0), ("YT", 1), ("XC", 5, "S"),
-    ("WT", 4), ("WQ", 0, 1), ("WT", 5), ("YC", 1, "S"), ("E", 2, 1),
-    ("S1", 3, 0, 0), ("S1", 3, 0, 1), ("XQ", 4), ("S1", 3, 1, 0), ("WC", 4, "S"),
-    ("XQ", 5), ("S1", 3, 1, 1), ("YQ", 1), ("XT", 6), ("WC", 5, "S"),
-    ("E", 3, 0), ("YT", 2), ("XC", 6, "S"), ("E", 3, 1), ("WT", 6),
-    ("WT", 7), ("YC", 2, "S"), ("XQ", 6), ("S1", 4, 0, 0), ("WC", 6, "V"),
-    ("S1", 4, 0, 1), ("S1", 4, 1, 0), ("E", 4, 0), ("S1", 4, 1, 1), ("WC", 7, "S"),
-    ("XT", 7), ("YQ", 2), ("YT", 3), ("WQ", 1, 0), ("XC", 7, "S"),
-    ("S1", 5, 0, 0), ("WQ", 1, 1), ("YC", 3, "S"), ("S1", 5, 0, 1), ("S1", 5, 1, 0),
-    ("E", 4, 1), ("S1", 5, 1, 1), ("S2", 0, 0), ("E", 5, 0), ("S2", 0, 1),
-    ("OC", 0, 0, "S"), ("YQ", 3), ("YT", 4), ("E", 5, 1), ("OC", 0, 1, "S"),
-    ("XQ", 7), ("S1", 6, 0, 0), ("YC", 4, "S"), ("S1", 6, 0, 1), ("ST", 0),
-    ("S1", 6, 1, 0), ("E", 6, 0), ("S1", 6, 1, 1), ("S2", 1, 0), ("E", 6, 1),
-    ("S2", 1, 1), ("OC", 1, 0, "S"), ("YQ", 4), ("YT", 5), ("OC", 1, 1, "S"),
-    ("S1", 7, 0, 0), ("YC", 5, "S"), ("S1", 7, 0, 1), ("ST", 1), ("S1", 7, 1, 0),
-    ("E", 7, 0), ("S1", 7, 1, 1), ("S2", 2, 0), ("E", 7, 1), ("S2", 2, 1),
-    ("OC", 2, 0, "S"), ("YQ", 5), ("YT", 6), ("OC", 2, 1, "S"), ("S2", 3, 0),
-    ("YC", 6, "S"), ("ST", 2), ("S2", 3, 1), ("OC", 3, 0, "V"), ("YT", 7),
-    ("OC", 3, 1, "S"), ("YQ", 6), ("S2", 4, 0), ("YC", 7, "S"), ("ST", 3),
-    ("S2", 4, 1), ("OC", 4, 0, "V"), ("S2", 5, 0), ("OC", 4, 1, "S"), ("YQ", 7),
-    ("S2", 5, 1), ("OC", 5, 0, "S"), ("ST", 4), ("S2", 6, 0), ("OC", 5, 1, "V"),
-    ("S2", 6, 1), ("OC", 6, 0, "S"), ("ST", 5), ("S2", 7, 0), ("OC", 6, 1, "S"),
-    ("S2", 7, 1), ("OC", 7, 0, "V"), ("ST", 6), ("OC", 7, 1, "S"), ("ST", 7),
-]
+FLOPS = 2 * 2 * SIZE * SIZE * SIZE
 
 
 def tile_precomputedmetanet_pb_kernel(tc, transformed, coeff, task_mat, Wp, out):
@@ -62,182 +30,306 @@ def tile_precomputedmetanet_pb_kernel(tc, transformed, coeff, task_mat, Wp, out)
         psum = ctx.enter_context(tc.psum_pool(name="psum", bufs=8))
         ctx.enter_context(tc.manual_schedule())
 
-        ident_b = keep.tile([P, P], BF16, name="ident_b")
-        ident_f = keep.tile([P, P], F32, name="ident_f")
-        c_bf = keep.tile([P, 8], BF16, name="c_bf")
-        c_sb = keep.tile([P, 8], F32, name="c_sb")
-        make_identity(nc, ident_b[:])
-        make_identity(nc, ident_f[:])
+        ident_bf16 = keep.tile([P, P], BF16, name="ident_bf16")
+        ident_f32 = keep.tile([P, P], F32, name="ident_f32")
+        coeff_bf16 = keep.tile([P, TILES], BF16, name="coeff_bf16")
+        coeff_f32 = keep.tile([P, TILES], F32, name="coeff_f32")
 
-        traw = keep.tile([P, 2, 4, 1024], BF16, name="traw")
-        tcod = keep.tile([P, 2, 1024], U32, name="tcod", align_bytes=64)
-        tscl = keep.tile([P, 2, 1024], U8, name="tscl", align_bytes=64)
-        wraw = keep.tile([P, 8, 1024], BF16, name="wraw")
-        wcod = keep.tile([P, 2, 1024], U32, name="wcod", align_bytes=64)
-        wscl = keep.tile([P, 2, 1024], U8, name="wscl", align_bytes=64)
-        tgrp = {}
+        x_raw = keep.tile([P, TILES, SIZE], BF16, name="x_raw")
+        t_raw = keep.tile([P, 2, PACK, SIZE], BF16, name="t_raw")
+        w_raw = keep.tile([P, TILES, SIZE], BF16, name="w_raw")
+        t_grouped = {}
         for g in range(2):
-            for c in range(2):
-                tgrp[(g, c)] = keep.tile([P, 512, 4], BF16, name="tgrp%d%d" % (g, c), align_bytes=64)
-        wgrp = [keep.tile([P, 2, 2048], BF16, name="wgrp%d" % c, align_bytes=64) for c in range(2)]
-        x_all = keep.tile([P, 8, 1024], BF16, name="x_all")
-        x_sb = [x_all[:, i, :] for i in range(8)]
-        x_dram = transformed.rearrange("(p i) d -> p i d", i=8)
-        out_dram = out.rearrange("(p i) o -> p i o", i=8)
-        xgrp = [keep.tile([P, 1024], BF16, name="xgrp%d" % i, align_bytes=64) for i in range(8)]
-        xcod = [keep.tile([P, 256], U32, name="xcod%d" % i, align_bytes=64) for i in range(8)]
-        xscl = [keep.tile([P, 256], U8, name="xscl%d" % i, align_bytes=64) for i in range(8)]
-        y_sb = [keep.tile([P, 2, 512], BF16, name="y_sb%d" % i) for i in range(8)]
-        ygrp = [keep.tile([P, 1024], BF16, name="ygrp%d" % i, align_bytes=64) for i in range(8)]
-        ycod = [keep.tile([P, 256], U32, name="ycod%d" % i, align_bytes=64) for i in range(8)]
-        yscl = [keep.tile([P, 256], U8, name="yscl%d" % i, align_bytes=64) for i in range(8)]
-        obuf = [keep.tile([P, 1024], F32, name="obuf%d" % i) for i in range(8)]
-        bank = {}
+            for h in range(2):
+                t_grouped[(g, h)] = keep.tile([P, HALF, PACK], BF16, name="t_grouped%d%d" % (g, h), align_bytes=64)
+        w_grouped = [keep.tile([P, 2, HALF * PACK], BF16, name="w_grouped%d" % h, align_bytes=64) for h in range(2)]
+        x_grouped = [keep.tile([P, 2 * P * PACK], BF16, name="x_grouped%d" % i, align_bytes=64) for i in range(TILES)]
+        y_grouped = [keep.tile([P, 2 * P * PACK], BF16, name="y_grouped%d" % i, align_bytes=64) for i in range(TILES)]
+        t_codes = keep.tile([P, 2, SIZE], U32, name="t_codes", align_bytes=64)
+        t_plane = keep.tile([P, 2, SIZE], U8, name="t_plane", align_bytes=64)
+        w_codes = keep.tile([P, 2, SIZE], U32, name="w_codes", align_bytes=64)
+        w_plane = keep.tile([P, 2, SIZE], U8, name="w_plane", align_bytes=64)
+        x_codes = [keep.tile([P, 2 * P], U32, name="x_codes%d" % i, align_bytes=64) for i in range(TILES)]
+        x_plane = [keep.tile([P, 2 * P], U8, name="x_plane%d" % i, align_bytes=64) for i in range(TILES)]
+        y_codes = [keep.tile([P, 2 * P], U32, name="y_codes%d" % i, align_bytes=64) for i in range(TILES)]
+        y_plane = [keep.tile([P, 2 * P], U8, name="y_plane%d" % i, align_bytes=64) for i in range(TILES)]
+        y_rows = [keep.tile([P, 2, SIZE // 2], BF16, name="y_rows%d" % i) for i in range(TILES)]
+        out_rows = [keep.tile([P, SIZE], F32, name="out_rows%d" % i) for i in range(TILES)]
 
-        def copy(eng, dst, src):
-            if eng == "V":
+        x_dram = transformed.rearrange("(p i) k -> p i k", i=TILES)
+        out_dram = out.rearrange("(p i) o -> p i o", i=TILES)
+        banks = {}
+
+        def new_bank(key, shape, dtype):
+            banks[key] = psum.tile(shape, dtype, name="bank", tag="bank")
+            return banks[key]
+
+        def copy(engine, dst, src):
+            if engine == "vector":
                 nc.vector.tensor_copy(out=dst, in_=src)
             else:
                 nc.scalar.copy(out=dst, in_=src)
 
-        def new_bank(key, shape, dtype):
-            t = psum.tile(shape, dtype, name="ps", tag="ps")
-            bank[key] = t
-            return t
+        def load_coeff():
+            nc.scalar.dma_start(out=coeff_bf16[:], in_=coeff.rearrange("(p i) -> p i", i=TILES))
 
-        def op_lc():
-            nc.scalar.dma_start(out=c_bf[:], in_=coeff.rearrange("(p i) -> p i", i=8))
-
-        def op_lt(g, u):
-            r0 = 512 * g + 256 * u
+        def load_task_rows(g, u):
+            first = HALF * g + 2 * P * u
             nc.sync.dma_start(
-                out=traw[:, g, 2 * u : 2 * u + 2, :],
-                in_=task_mat[r0 : r0 + 256, :].rearrange("(p e) d -> p e d", e=2),
+                out=t_raw[:, g, 2 * u : 2 * u + 2, :],
+                in_=task_mat[first : first + 2 * P, :].rearrange("(p e) d -> p e d", e=2),
             )
 
-        def op_lx(a):
-            nc.sync.dma_start(out=x_all[:, 2 * a : 2 * a + 2, :], in_=x_dram[:, 2 * a : 2 * a + 2, :])
+        def load_x_pair(a):
+            nc.sync.dma_start(out=x_raw[:, 2 * a : 2 * a + 2, :], in_=x_dram[:, 2 * a : 2 * a + 2, :])
 
-        def op_lw(c):
+        def load_w_half(h):
             nc.sync.dma_start(
-                out=wraw[:, 4 * c : 4 * c + 4, :],
-                in_=Wp[512 * c : 512 * c + 512, :].rearrange("(j p) d -> p j d", p=P),
+                out=w_raw[:, 4 * h : 4 * h + 4, :],
+                in_=Wp[HALF * h : HALF * h + HALF, :].rearrange("(j p) k -> p j k", p=P),
             )
 
-        def op_cc():
-            nc.vector.tensor_copy(out=c_sb[:], in_=c_bf[:])
+        def store(i):
+            nc.sync.dma_start(out=out_dram[:, i, :], in_=out_rows[i][:])
 
-        def regroup(eng, g, c, lo, hi):
-            src = traw[:, g, :, 512 * c + lo : 512 * c + hi].rearrange("p t (c i) -> p c t i", i=4)
-            dst = tgrp[(g, c)][:, lo:hi, :].rearrange("p (c i) t -> p c t i", i=4)
-            copy(eng, dst, src)
+        def regroup_task(engine, g, h):
+            lo, hi = (0, VECTOR_COLUMNS) if engine == "vector" else (VECTOR_COLUMNS, HALF)
+            src = t_raw[:, g, :, HALF * h + lo : HALF * h + hi].rearrange("p t (c i) -> p c t i", i=4)
+            dst = t_grouped[(g, h)][:, lo:hi, :].rearrange("p (c i) t -> p c t i", i=4)
+            copy(engine, dst, src)
 
-        def op_rv(g, c):
-            regroup("V", g, c, 0, VCOLS)
-
-        def op_rs(g, c):
-            regroup("S", g, c, VCOLS, 512)
-
-        def op_qt(g, c):
+        def quantise_task(g, h):
+            cols = slice(HALF * h, HALF * h + HALF)
             nc.vector.quantize_mx(
-                out=tcod[:, g, 512 * c : 512 * c + 512].bitcast(FP8X4),
-                scales=tscl[:, g, 512 * c : 512 * c + 512],
-                in_=tgrp[(g, c)][:].rearrange("p d t -> p (d t)"),
+                out=t_codes[:, g, cols].bitcast(FP8X4),
+                scales=t_plane[:, g, cols],
+                in_=t_grouped[(g, h)][:].rearrange("p d t -> p (d t)"),
             )
 
-        def word_transposes(key, rows):
-            t = new_bank(key, [P, 4, P], F32)
+        def transpose_words(key, rows):
+            bank = new_bank(key, [P, PACK, P], F32)
             words = rows.bitcast(F32)
-            for q in range(4):
-                nc.tensor.transpose(t[:, q, :], words[:, P * q : P * q + P], ident_f[:])
+            for block in range(PACK):
+                nc.tensor.transpose(bank[:, block, :], words[:, P * block : P * block + P], ident_f32[:])
 
-        def op_xt(i):
-            word_transposes(("x", i), x_sb[i][:])
+        def words_out(key):
+            return banks[key][:].rearrange("p (g u) r -> p g r u", g=2, u=2)
 
-        def op_xc(i, eng):
-            dst = xgrp[i][:].bitcast(F32).rearrange("p (g b u) -> p g b u", g=2, b=P, u=2)
-            copy(eng, dst, bank[("x", i)][:].rearrange("p (g u) b -> p g b u", g=2, u=2))
+        def transpose_x(i):
+            transpose_words(("x", i), x_raw[:, i, :])
 
-        def op_xq(i):
-            nc.vector.quantize_mx(out=xcod[i][:].bitcast(FP8X4), scales=xscl[i][:], in_=xgrp[i][:])
+        def copy_x(i):
+            dst = x_grouped[i][:].bitcast(F32).rearrange("p (g r u) -> p g r u", g=2, r=P, u=2)
+            copy("scalar", dst, words_out(("x", i)))
 
-        def op_s1(i, c, g):
-            if g == 0:
-                new_bank(("z", i, c), [P, 512], F32)
+        def quantise_x(i):
+            nc.vector.quantize_mx(out=x_codes[i][:].bitcast(FP8X4), scales=x_plane[i][:], in_=x_grouped[i][:])
+
+        def transpose_w(j):
+            transpose_words(("w", j), w_raw[:, j, :])
+
+        def copy_w(j):
+            lo = P * (j % 4)
+            dst = w_grouped[j // 4][:].bitcast(F32).rearrange("p g (r u) -> p g r u", u=2)
+            copy("scalar", dst[:, :, lo : lo + P, :], words_out(("w", j)))
+
+        def quantise_w(h, g):
+            cols = slice(HALF * h, HALF * h + HALF)
+            nc.vector.quantize_mx(
+                out=w_codes[:, g, cols].bitcast(FP8X4), scales=w_plane[:, g, cols], in_=w_grouped[h][:, g, :]
+            )
+
+        def mx_pass(bank, codes, plane, moving_codes, moving_plane, g, h):
+            cols = slice(HALF * h, HALF * h + HALF)
             nc.tensor.matmul_mx(
-                out=bank[("z", i, c)][:],
-                lhsT=xcod[i][:, P * g : P * g + P].bitcast(FP8X4),
-                lhsT_scale=xscl[i][:, P * g : P * g + P],
-                rhs=tcod[:, g, 512 * c : 512 * c + 512].bitcast(FP8X4),
-                rhs_scale=tscl[:, g, 512 * c : 512 * c + 512],
+                out=bank[:],
+                lhsT=codes[:, P * g : P * g + P].bitcast(FP8X4),
+                lhsT_scale=plane[:, P * g : P * g + P],
+                rhs=moving_codes[:, g, cols].bitcast(FP8X4),
+                rhs_scale=moving_plane[:, g, cols],
                 start=(g == 0),
                 stop=(g == 1),
             )
 
-        def op_e(i, c):
+        def product1_pass(i, h, g):
+            bank = new_bank(("z", i, h), [P, HALF], F32) if g == 0 else banks[("z", i, h)]
+            mx_pass(bank, x_codes[i], x_plane[i], t_codes, t_plane, g, h)
+
+        def product1(i):
+            for h in range(2):
+                for g in range(2):
+                    product1_pass(i, h, g)
+
+        def step(i, h):
             nc.vector.scalar_tensor_tensor(
-                out=y_sb[i][:, :, 256 * c : 256 * c + 256],
-                in0=bank[("z", i, c)][:].rearrange("p (w e) -> p e w", e=2),
-                scalar=c_sb[:, i : i + 1],
-                in1=x_sb[i][:, 512 * c : 512 * c + 512].rearrange("p (w e) -> p e w", e=2),
+                out=y_rows[i][:, :, HALF // 2 * h : HALF // 2 * (h + 1)],
+                in0=banks[("z", i, h)][:].rearrange("p (w e) -> p e w", e=2),
+                scalar=coeff_f32[:, i : i + 1],
+                in1=x_raw[:, i, HALF * h : HALF * h + HALF].rearrange("p (w e) -> p e w", e=2),
                 op0=MULT,
                 op1=ADD,
             )
 
-        def op_yt(i):
-            t = new_bank(("y", i), [P, 8, P], BF16)
+        def steps(i):
+            step(i, 0)
+            step(i, 1)
+
+        def transpose_y(i):
+            bank = new_bank(("y", i), [P, 2 * PACK, P], BF16)
             for g in range(2):
                 for u in range(2):
                     for e in range(2):
-                        q = 2 * g + u
-                        nc.tensor.transpose(t[:, 4 * g + 2 * u + e, :], y_sb[i][:, e, P * q : P * q + P], ident_b[:])
+                        block = 2 * g + u
+                        nc.tensor.transpose(
+                            bank[:, PACK * g + 2 * u + e, :], y_rows[i][:, e, P * block : P * block + P], ident_bf16[:]
+                        )
 
-        def op_yc(i, eng):
-            dst = ygrp[i][:].rearrange("p (g b t) -> p g b t", g=2, b=P, t=4)
-            copy(eng, dst, bank[("y", i)][:].rearrange("p (g t) b -> p g b t", g=2, t=4))
+        def copy_y(i, engine):
+            dst = y_grouped[i][:].rearrange("p (g r t) -> p g r t", g=2, r=P, t=PACK)
+            copy(engine, dst, banks[("y", i)][:].rearrange("p (g t) r -> p g r t", g=2, t=PACK))
 
-        def op_yq(i):
-            nc.vector.quantize_mx(out=ycod[i][:].bitcast(FP8X4), scales=yscl[i][:], in_=ygrp[i][:])
+        def quantise_y(i):
+            nc.vector.quantize_mx(out=y_codes[i][:].bitcast(FP8X4), scales=y_plane[i][:], in_=y_grouped[i][:])
 
-        def op_wt(j):
-            word_transposes(("w", j), wraw[:, j, :])
-
-        def op_wc(j, eng):
-            lo = P * (j % 4)
-            dst = wgrp[j // 4][:].bitcast(F32).rearrange("p g (o u) -> p g o u", u=2)[:, :, lo : lo + P, :]
-            copy(eng, dst, bank[("w", j)][:].rearrange("p (g u) o -> p g o u", g=2, u=2))
-
-        def op_wq(c, g):
-            nc.vector.quantize_mx(
-                out=wcod[:, g, 512 * c : 512 * c + 512].bitcast(FP8X4),
-                scales=wscl[:, g, 512 * c : 512 * c + 512],
-                in_=wgrp[c][:, g, :],
-            )
-
-        def op_s2(i, c):
-            t = new_bank(("o", i, c), [P, 512], F32)
+        def product2(i, h):
+            bank = new_bank(("o", i, h), [P, HALF], F32)
             for g in range(2):
-                nc.tensor.matmul_mx(
-                    out=t[:],
-                    lhsT=ycod[i][:, P * g : P * g + P].bitcast(FP8X4),
-                    lhsT_scale=yscl[i][:, P * g : P * g + P],
-                    rhs=wcod[:, g, 512 * c : 512 * c + 512].bitcast(FP8X4),
-                    rhs_scale=wscl[:, g, 512 * c : 512 * c + 512],
-                    start=(g == 0),
-                    stop=(g == 1),
-                )
+                mx_pass(bank, y_codes[i], y_plane[i], w_codes, w_plane, g, h)
 
-        def op_oc(i, c, eng):
-            copy(eng, obuf[i][:, 512 * c : 512 * c + 512], bank[("o", i, c)][:])
+        def copy_out(i, h, engine):
+            copy(engine, out_rows[i][:, HALF * h : HALF * h + HALF], banks[("o", i, h)][:])
 
-        def op_st(i):
-            nc.sync.dma_start(out=out_dram[:, i, :], in_=obuf[i][:])
+        def finish(i):
+            product2(i, 0)
+            product2(i, 1)
+            copy_out(i, 0, "vector")
+            copy_out(i, 1, "scalar")
+            store(i)
 
-        ops = {
-            "LC": op_lc, "LT": op_lt, "LX": op_lx, "LW": op_lw, "CC": op_cc,
-            "RV": op_rv, "RS": op_rs, "QT": op_qt, "XT": op_xt, "XC": op_xc, "XQ": op_xq,
-            "S1": op_s1, "E": op_e, "YT": op_yt, "YC": op_yc, "YQ": op_yq,
-            "WT": op_wt, "WC": op_wc, "WQ": op_wq, "S2": op_s2, "OC": op_oc, "ST": op_st,
-        }
-        for step in ORDER:
-            ops[step[0]](*step[1:])
+        make_identity(nc, ident_bf16[:])
+        make_identity(nc, ident_f32[:])
+
+        load_coeff()
+        load_task_rows(0, 0)
+        load_task_rows(0, 1)
+        load_x_pair(0)
+        load_task_rows(1, 0)
+        load_task_rows(1, 1)
+        load_x_pair(1)
+        load_x_pair(2)
+        load_w_half(0)
+        load_x_pair(3)
+        load_w_half(1)
+        nc.vector.tensor_copy(out=coeff_f32[:], in_=coeff_bf16[:])
+
+        for h in range(2):
+            regroup_task("vector", 0, h)
+            regroup_task("scalar", 0, h)
+        for h in range(2):
+            quantise_task(0, h)
+
+        for i in (0, 1):
+            transpose_x(i)
+        for i in (0, 1):
+            copy_x(i)
+        for i in (0, 1):
+            quantise_x(i)
+
+        for i in (0, 1):
+            for h in range(2):
+                product1_pass(i, h, 0)
+
+        for h in range(2):
+            regroup_task("vector", 1, h)
+            regroup_task("scalar", 1, h)
+        for h in range(2):
+            quantise_task(1, h)
+
+        for i in (2, 3, 4, 5):
+            transpose_x(i)
+        for i in (2, 3, 4, 5):
+            copy_x(i)
+        quantise_x(2)
+
+        for i in (0, 1):
+            for h in range(2):
+                product1_pass(i, h, 1)
+        product1(2)
+        for i in FIRST:
+            steps(i)
+
+        for j in (0, 1):
+            transpose_w(j)
+            transpose_y(j)
+        transpose_w(2)
+        transpose_w(3)
+        transpose_y(2)
+        transpose_x(6)
+        for j in (4, 5, 6, 7):
+            transpose_w(j)
+        transpose_x(7)
+
+        for j in (0, 1):
+            copy_w(j)
+            copy_y(j, "scalar")
+        copy_w(2)
+        copy_w(3)
+        copy_x(6)
+        for j in (4, 5, 6, 7):
+            copy_w(j)
+        copy_x(7)
+
+        quantise_x(3)
+        quantise_x(4)
+        quantise_y(0)
+        quantise_x(5)
+        copy_y(2, "vector")
+        for g in range(2):
+            quantise_w(0, g)
+        quantise_y(1)
+        quantise_y(2)
+
+        product1(3)
+        product1(4)
+        for i in FIRST:
+            product2(i, 0)
+        product1(5)
+
+        steps(3)
+        for g in range(2):
+            quantise_w(1, g)
+        steps(4)
+        step(5, 0)
+        quantise_x(6)
+        quantise_x(7)
+        step(5, 1)
+        for i in FIRST:
+            copy_out(i, 0, "scalar")
+
+        for i in FIRST:
+            product2(i, 1)
+        product1(6)
+        product1(7)
+
+        for i in FIRST:
+            copy_out(i, 1, "scalar")
+            store(i)
+        steps(6)
+        steps(7)
+
+        for i in REST:
+            transpose_y(i)
+        copy_y(3, "scalar")
+        copy_y(4, "vector")
+        quantise_y(3)
+        quantise_y(4)
+        copy_y(5, "scalar")
+        copy_y(6, "vector")
+        quantise_y(5)
+        copy_y(7, "scalar")
+
+        finish(3)
+        quantise_y(6)
+        quantise_y(7)
+        for i in (4, 5, 6, 7):
+            finish(i)

@@ -18,6 +18,7 @@ HALF = 512
 PACK = 4
 FIRST = (0, 1, 2)
 REST = (3, 4, 5, 6, 7)
+BOTH = (0, 1)
 VECTOR_COLUMNS = 352
 
 FLOPS = 2 * 2 * SIZE * SIZE * SIZE
@@ -128,10 +129,10 @@ def tile_precomputedmetanet_pb_kernel(tc, transformed, coeff, task_mat, Wp, out)
         def transpose_w(j):
             transpose_words(("w", j), w_raw[:, j, :])
 
-        def copy_w(j):
+        def copy_w(j, engine):
             lo = P * (j % 4)
             dst = w_grouped[j // 4][:].bitcast(F32).rearrange("p g (r u) -> p g r u", u=2)
-            copy("scalar", dst[:, :, lo : lo + P, :], words_out(("w", j)))
+            copy(engine, dst[:, :, lo : lo + P, :], words_out(("w", j)))
 
         def quantise_w(h, g):
             cols = slice(HALF * h, HALF * h + HALF)
@@ -174,19 +175,20 @@ def tile_precomputedmetanet_pb_kernel(tc, transformed, coeff, task_mat, Wp, out)
             step(i, 0)
             step(i, 1)
 
-        def transpose_y(i):
-            bank = new_bank(("y", i), [P, 2 * PACK, P], BF16)
-            for g in range(2):
+        def transpose_y(i, passes):
+            bank = new_bank(("y", i, passes), [P, len(passes) * PACK, P], BF16)
+            for n, g in enumerate(passes):
                 for u in range(2):
                     for e in range(2):
                         block = 2 * g + u
                         nc.tensor.transpose(
-                            bank[:, PACK * g + 2 * u + e, :], y_rows[i][:, e, P * block : P * block + P], ident_bf16[:]
+                            bank[:, PACK * n + 2 * u + e, :], y_rows[i][:, e, P * block : P * block + P], ident_bf16[:]
                         )
 
-        def copy_y(i, engine):
+        def copy_y(i, passes, engine):
             dst = y_grouped[i][:].rearrange("p (g r t) -> p g r t", g=2, r=P, t=PACK)
-            copy(engine, dst, banks[("y", i)][:].rearrange("p (g t) r -> p g r t", g=2, t=PACK))
+            src = banks[("y", i, passes)][:].rearrange("p (g t) r -> p g r t", g=len(passes), t=PACK)
+            copy(engine, dst[:, passes[0] : passes[-1] + 1, :, :], src)
 
         def quantise_y(i):
             nc.vector.quantize_mx(out=y_codes[i][:].bitcast(FP8X4), scales=y_plane[i][:], in_=y_grouped[i][:])
@@ -199,10 +201,10 @@ def tile_precomputedmetanet_pb_kernel(tc, transformed, coeff, task_mat, Wp, out)
         def copy_out(i, h, engine):
             copy(engine, out_rows[i][:, HALF * h : HALF * h + HALF], banks[("o", i, h)][:])
 
-        def finish(i):
+        def finish(i, engine0):
             product2(i, 0)
             product2(i, 1)
-            copy_out(i, 0, "vector")
+            copy_out(i, 0, engine0)
             copy_out(i, 1, "scalar")
             store(i)
 
@@ -260,30 +262,30 @@ def tile_precomputedmetanet_pb_kernel(tc, transformed, coeff, task_mat, Wp, out)
 
         for j in (0, 1):
             transpose_w(j)
-            transpose_y(j)
+            transpose_y(j, BOTH)
         transpose_w(2)
         transpose_w(3)
-        transpose_y(2)
+        transpose_y(2, BOTH)
         transpose_x(6)
         for j in (4, 5, 6, 7):
             transpose_w(j)
         transpose_x(7)
 
         for j in (0, 1):
-            copy_w(j)
-            copy_y(j, "scalar")
-        copy_w(2)
-        copy_w(3)
+            copy_w(j, "scalar")
+            copy_y(j, BOTH, "scalar")
+        copy_w(3, "scalar")
         copy_x(6)
         for j in (4, 5, 6, 7):
-            copy_w(j)
+            copy_w(j, "scalar")
         copy_x(7)
 
         quantise_x(3)
         quantise_x(4)
         quantise_y(0)
         quantise_x(5)
-        copy_y(2, "vector")
+        copy_w(2, "vector")
+        copy_y(2, BOTH, "vector")
         for g in range(2):
             quantise_w(0, g)
         quantise_y(1)
@@ -318,18 +320,15 @@ def tile_precomputedmetanet_pb_kernel(tc, transformed, coeff, task_mat, Wp, out)
         steps(7)
 
         for i in REST:
-            transpose_y(i)
-        copy_y(3, "scalar")
-        copy_y(4, "vector")
-        quantise_y(3)
-        quantise_y(4)
-        copy_y(5, "scalar")
-        copy_y(6, "vector")
-        quantise_y(5)
-        copy_y(7, "scalar")
+            for g in BOTH:
+                transpose_y(i, (g,))
+        for n, i in enumerate(REST):
+            copy_y(i, (0,), "scalar")
+            copy_y(i, (1,), "vector")
+            if n > 0:
+                quantise_y(REST[n - 1])
+        quantise_y(REST[-1])
 
-        finish(3)
-        quantise_y(6)
-        quantise_y(7)
-        for i in (4, 5, 6, 7):
-            finish(i)
+        finish(REST[0], "scalar")
+        for i in REST[1:]:
+            finish(i, "vector")

@@ -18,7 +18,6 @@ HALF = 512
 PACK = 4
 FIRST = (0, 1, 2)
 REST = (3, 4, 5, 6, 7)
-BOTH = (0, 1)
 VECTOR_COLUMNS = 352
 
 FLOPS = 2 * 2 * SIZE * SIZE * SIZE
@@ -175,20 +174,19 @@ def tile_precomputedmetanet_pb_kernel(tc, transformed, coeff, task_mat, Wp, out)
             step(i, 0)
             step(i, 1)
 
-        def transpose_y(i, passes):
-            bank = new_bank(("y", i, passes), [P, len(passes) * PACK, P], BF16)
-            for n, g in enumerate(passes):
+        def transpose_y(i):
+            bank = new_bank(("y", i), [P, 2 * PACK, P], BF16)
+            for g in range(2):
                 for u in range(2):
                     for e in range(2):
                         block = 2 * g + u
                         nc.tensor.transpose(
-                            bank[:, PACK * n + 2 * u + e, :], y_rows[i][:, e, P * block : P * block + P], ident_bf16[:]
+                            bank[:, PACK * g + 2 * u + e, :], y_rows[i][:, e, P * block : P * block + P], ident_bf16[:]
                         )
 
-        def copy_y(i, passes, engine):
+        def copy_y(i, engine):
             dst = y_grouped[i][:].rearrange("p (g r t) -> p g r t", g=2, r=P, t=PACK)
-            src = banks[("y", i, passes)][:].rearrange("p (g t) r -> p g r t", g=len(passes), t=PACK)
-            copy(engine, dst[:, passes[0] : passes[-1] + 1, :, :], src)
+            copy(engine, dst, banks[("y", i)][:].rearrange("p (g t) r -> p g r t", g=2, t=PACK))
 
         def quantise_y(i):
             nc.vector.quantize_mx(out=y_codes[i][:].bitcast(FP8X4), scales=y_plane[i][:], in_=y_grouped[i][:])
@@ -201,10 +199,10 @@ def tile_precomputedmetanet_pb_kernel(tc, transformed, coeff, task_mat, Wp, out)
         def copy_out(i, h, engine):
             copy(engine, out_rows[i][:, HALF * h : HALF * h + HALF], banks[("o", i, h)][:])
 
-        def finish(i, engine0):
+        def finish(i):
             product2(i, 0)
             product2(i, 1)
-            copy_out(i, 0, engine0)
+            copy_out(i, 0, "vector")
             copy_out(i, 1, "scalar")
             store(i)
 
@@ -262,10 +260,10 @@ def tile_precomputedmetanet_pb_kernel(tc, transformed, coeff, task_mat, Wp, out)
 
         for j in (0, 1):
             transpose_w(j)
-            transpose_y(j, BOTH)
+            transpose_y(j)
         transpose_w(2)
         transpose_w(3)
-        transpose_y(2, BOTH)
+        transpose_y(2)
         transpose_x(6)
         for j in (4, 5, 6, 7):
             transpose_w(j)
@@ -273,7 +271,7 @@ def tile_precomputedmetanet_pb_kernel(tc, transformed, coeff, task_mat, Wp, out)
 
         for j in (0, 1):
             copy_w(j, "scalar")
-            copy_y(j, BOTH, "scalar")
+            copy_y(j, "scalar")
         copy_w(3, "scalar")
         copy_x(6)
         for j in (4, 5, 6, 7):
@@ -285,7 +283,7 @@ def tile_precomputedmetanet_pb_kernel(tc, transformed, coeff, task_mat, Wp, out)
         quantise_y(0)
         quantise_x(5)
         copy_w(2, "vector")
-        copy_y(2, BOTH, "vector")
+        copy_y(2, "vector")
         for g in range(2):
             quantise_w(0, g)
         quantise_y(1)
@@ -320,15 +318,18 @@ def tile_precomputedmetanet_pb_kernel(tc, transformed, coeff, task_mat, Wp, out)
         steps(7)
 
         for i in REST:
-            for g in BOTH:
-                transpose_y(i, (g,))
-        for n, i in enumerate(REST):
-            copy_y(i, (0,), "scalar")
-            copy_y(i, (1,), "vector")
-            if n > 0:
-                quantise_y(REST[n - 1])
-        quantise_y(REST[-1])
+            transpose_y(i)
+        copy_y(3, "scalar")
+        copy_y(4, "vector")
+        quantise_y(3)
+        quantise_y(4)
+        copy_y(5, "scalar")
+        copy_y(6, "vector")
+        quantise_y(5)
+        copy_y(7, "scalar")
 
-        finish(REST[0], "scalar")
-        for i in REST[1:]:
-            finish(i, "vector")
+        finish(3)
+        quantise_y(6)
+        quantise_y(7)
+        for i in (4, 5, 6, 7):
+            finish(i)

from contextlib import ExitStack

import concourse.mybir as mybir
from concourse.masks import make_identity

F32 = mybir.dt.float32
BF16 = mybir.dt.bfloat16
U32 = mybir.dt.uint32
U8 = mybir.dt.uint8
FP8X4 = mybir.dt.float8_e4m3fn_x4
MULT = mybir.AluOpType.mult
ADD = mybir.AluOpType.add

P = 128
SIZE = 1024
TILES = SIZE // P
HALF = 512
PACK = 4
FIRST = (0, 1, 2)
REST = (3, 4, 5, 6, 7)
VECTOR_COLUMNS = 352

FLOPS = 2 * 2 * SIZE * SIZE * SIZE


def tile_precomputedmetanet_pb_kernel(tc, transformed, coeff, task_mat, Wp, out):
    nc = tc.nc
    with ExitStack() as ctx:
        keep = ctx.enter_context(tc.tile_pool(name="keep", bufs=1))
        psum = ctx.enter_context(tc.psum_pool(name="psum", bufs=8))
        ctx.enter_context(tc.manual_schedule())

        ident_bf16 = keep.tile([P, P], BF16, name="ident_bf16")
        ident_f32 = keep.tile([P, P], F32, name="ident_f32")
        coeff_bf16 = keep.tile([P, TILES], BF16, name="coeff_bf16")
        coeff_f32 = keep.tile([P, TILES], F32, name="coeff_f32")

        x_raw = keep.tile([P, TILES, SIZE], BF16, name="x_raw")
        t_raw = keep.tile([P, 2, PACK, SIZE], BF16, name="t_raw")
        w_raw = keep.tile([P, TILES, SIZE], BF16, name="w_raw")
        t_grouped = {}
        for g in range(2):
            for h in range(2):
                t_grouped[(g, h)] = keep.tile([P, HALF, PACK], BF16, name="t_grouped%d%d" % (g, h), align_bytes=64)
        w_grouped = [keep.tile([P, 2, HALF * PACK], BF16, name="w_grouped%d" % h, align_bytes=64) for h in range(2)]
        x_grouped = [keep.tile([P, 2 * P * PACK], BF16, name="x_grouped%d" % i, align_bytes=64) for i in range(TILES)]
        y_grouped = [keep.tile([P, 2 * P * PACK], BF16, name="y_grouped%d" % i, align_bytes=64) for i in range(TILES)]
        t_codes = keep.tile([P, 2, SIZE], U32, name="t_codes", align_bytes=64)
        t_plane = keep.tile([P, 2, SIZE], U8, name="t_plane", align_bytes=64)
        w_codes = keep.tile([P, 2, SIZE], U32, name="w_codes", align_bytes=64)
        w_plane = keep.tile([P, 2, SIZE], U8, name="w_plane", align_bytes=64)
        x_codes = [keep.tile([P, 2 * P], U32, name="x_codes%d" % i, align_bytes=64) for i in range(TILES)]
        x_plane = [keep.tile([P, 2 * P], U8, name="x_plane%d" % i, align_bytes=64) for i in range(TILES)]
        y_codes = [keep.tile([P, 2 * P], U32, name="y_codes%d" % i, align_bytes=64) for i in range(TILES)]
        y_plane = [keep.tile([P, 2 * P], U8, name="y_plane%d" % i, align_bytes=64) for i in range(TILES)]
        y_rows = [keep.tile([P, 2, SIZE // 2], BF16, name="y_rows%d" % i) for i in range(TILES)]
        out_rows = [keep.tile([P, SIZE], F32, name="out_rows%d" % i) for i in range(TILES)]

        x_dram = transformed.rearrange("(p i) k -> p i k", i=TILES)
        out_dram = out.rearrange("(p i) o -> p i o", i=TILES)
        banks = {}

        def new_bank(key, shape, dtype):
            banks[key] = psum.tile(shape, dtype, name="bank", tag="bank")
            return banks[key]

        def copy(engine, dst, src):
            if engine == "vector":
                nc.vector.tensor_copy(out=dst, in_=src)
            else:
                nc.scalar.copy(out=dst, in_=src)

        def load_coeff():
            nc.scalar.dma_start(out=coeff_bf16[:], in_=coeff.rearrange("(p i) -> p i", i=TILES))

        def load_task_rows(g, u):
            first = HALF * g + 2 * P * u
            nc.sync.dma_start(
                out=t_raw[:, g, 2 * u : 2 * u + 2, :],
                in_=task_mat[first : first + 2 * P, :].rearrange("(p e) d -> p e d", e=2),
            )

        def load_x_pair(a):
            nc.sync.dma_start(out=x_raw[:, 2 * a : 2 * a + 2, :], in_=x_dram[:, 2 * a : 2 * a + 2, :])

        def load_w_half(h):
            nc.sync.dma_start(
                out=w_raw[:, 4 * h : 4 * h + 4, :],
                in_=Wp[HALF * h : HALF * h + HALF, :].rearrange("(j p) k -> p j k", p=P),
            )

        def store(i):
            nc.sync.dma_start(out=out_dram[:, i, :], in_=out_rows[i][:])

        def regroup_task(engine, g, h):
            lo, hi = (0, VECTOR_COLUMNS) if engine == "vector" else (VECTOR_COLUMNS, HALF)
            src = t_raw[:, g, :, HALF * h + lo : HALF * h + hi].rearrange("p t (c i) -> p c t i", i=4)
            dst = t_grouped[(g, h)][:, lo:hi, :].rearrange("p (c i) t -> p c t i", i=4)
            copy(engine, dst, src)

        def quantise_task(g, h):
            cols = slice(HALF * h, HALF * h + HALF)
            nc.vector.quantize_mx(
                out=t_codes[:, g, cols].bitcast(FP8X4),
                scales=t_plane[:, g, cols],
                in_=t_grouped[(g, h)][:].rearrange("p d t -> p (d t)"),
            )

        def transpose_words(key, rows):
            bank = new_bank(key, [P, PACK, P], F32)
            words = rows.bitcast(F32)
            for block in range(PACK):
                nc.tensor.transpose(bank[:, block, :], words[:, P * block : P * block + P], ident_f32[:])

        def words_out(key):
            return banks[key][:].rearrange("p (g u) r -> p g r u", g=2, u=2)

        def transpose_x(i):
            transpose_words(("x", i), x_raw[:, i, :])

        def copy_x(i):
            dst = x_grouped[i][:].bitcast(F32).rearrange("p (g r u) -> p g r u", g=2, r=P, u=2)
            copy("scalar", dst, words_out(("x", i)))

        def quantise_x(i):
            nc.vector.quantize_mx(out=x_codes[i][:].bitcast(FP8X4), scales=x_plane[i][:], in_=x_grouped[i][:])

        def transpose_w(j):
            transpose_words(("w", j), w_raw[:, j, :])

        def copy_w(j, engine):
            lo = P * (j % 4)
            dst = w_grouped[j // 4][:].bitcast(F32).rearrange("p g (r u) -> p g r u", u=2)
            copy(engine, dst[:, :, lo : lo + P, :], words_out(("w", j)))

        def quantise_w(h, g):
            cols = slice(HALF * h, HALF * h + HALF)
            nc.vector.quantize_mx(
                out=w_codes[:, g, cols].bitcast(FP8X4), scales=w_plane[:, g, cols], in_=w_grouped[h][:, g, :]
            )

        def mx_pass(bank, codes, plane, moving_codes, moving_plane, g, h):
            cols = slice(HALF * h, HALF * h + HALF)
            nc.tensor.matmul_mx(
                out=bank[:],
                lhsT=codes[:, P * g : P * g + P].bitcast(FP8X4),
                lhsT_scale=plane[:, P * g : P * g + P],
                rhs=moving_codes[:, g, cols].bitcast(FP8X4),
                rhs_scale=moving_plane[:, g, cols],
                start=(g == 0),
                stop=(g == 1),
            )

        def product1_pass(i, h, g):
            bank = new_bank(("z", i, h), [P, HALF], F32) if g == 0 else banks[("z", i, h)]
            mx_pass(bank, x_codes[i], x_plane[i], t_codes, t_plane, g, h)

        def product1(i):
            for h in range(2):
                for g in range(2):
                    product1_pass(i, h, g)

        def step(i, h):
            nc.vector.scalar_tensor_tensor(
                out=y_rows[i][:, :, HALF // 2 * h : HALF // 2 * (h + 1)],
                in0=banks[("z", i, h)][:].rearrange("p (w e) -> p e w", e=2),
                scalar=coeff_f32[:, i : i + 1],
                in1=x_raw[:, i, HALF * h : HALF * h + HALF].rearrange("p (w e) -> p e w", e=2),
                op0=MULT,
                op1=ADD,
            )

        def steps(i):
            step(i, 0)
            step(i, 1)

        def transpose_y(i):
            bank = new_bank(("y", i), [P, 2 * PACK, P], BF16)
            for g in range(2):
                for u in range(2):
                    for e in range(2):
                        block = 2 * g + u
                        nc.tensor.transpose(
                            bank[:, PACK * g + 2 * u + e, :], y_rows[i][:, e, P * block : P * block + P], ident_bf16[:]
                        )

        def copy_y(i, engine):
            dst = y_grouped[i][:].rearrange("p (g r t) -> p g r t", g=2, r=P, t=PACK)
            copy(engine, dst, banks[("y", i)][:].rearrange("p (g t) r -> p g r t", g=2, t=PACK))

        def quantise_y(i):
            nc.vector.quantize_mx(out=y_codes[i][:].bitcast(FP8X4), scales=y_plane[i][:], in_=y_grouped[i][:])

        def product2(i, h):
            bank = new_bank(("o", i, h), [P, HALF], F32)
            for g in range(2):
                mx_pass(bank, y_codes[i], y_plane[i], w_codes, w_plane, g, h)

        def copy_out(i, h, engine):
            copy(engine, out_rows[i][:, HALF * h : HALF * h + HALF], banks[("o", i, h)][:])

        def finish(i):
            product2(i, 0)
            product2(i, 1)
            copy_out(i, 0, "vector")
            copy_out(i, 1, "scalar")
            store(i)

        make_identity(nc, ident_bf16[:])
        make_identity(nc, ident_f32[:])

        load_coeff()
        load_task_rows(0, 0)
        load_task_rows(0, 1)
        load_x_pair(0)
        load_task_rows(1, 0)
        load_task_rows(1, 1)
        load_x_pair(1)
        load_x_pair(2)
        load_w_half(0)
        load_x_pair(3)
        load_w_half(1)
        nc.vector.tensor_copy(out=coeff_f32[:], in_=coeff_bf16[:])

        for h in range(2):
            regroup_task("vector", 0, h)
            regroup_task("scalar", 0, h)
        for h in range(2):
            quantise_task(0, h)

        for i in (0, 1):
            transpose_x(i)
        for i in (0, 1):
            copy_x(i)
        for i in (0, 1):
            quantise_x(i)

        for i in (0, 1):
            for h in range(2):
                product1_pass(i, h, 0)

        for h in range(2):
            regroup_task("vector", 1, h)
            regroup_task("scalar", 1, h)
        for h in range(2):
            quantise_task(1, h)

        for i in (2, 3, 4, 5):
            transpose_x(i)
        for i in (2, 3, 4, 5):
            copy_x(i)
        quantise_x(2)

        for i in (0, 1):
            for h in range(2):
                product1_pass(i, h, 1)
        product1(2)
        for i in FIRST:
            steps(i)

        for j in (0, 1):
            transpose_w(j)
            transpose_y(j)
        transpose_w(2)
        transpose_w(3)
        transpose_y(2)
        transpose_x(6)
        for j in (4, 5, 6, 7):
            transpose_w(j)
        transpose_x(7)

        for j in (0, 1):
            copy_w(j, "scalar")
            copy_y(j, "scalar")
        copy_w(3, "scalar")
        copy_x(6)
        for j in (4, 5, 6, 7):
            copy_w(j, "scalar")
        copy_x(7)

        quantise_x(3)
        quantise_x(4)
        quantise_y(0)
        quantise_x(5)
        copy_w(2, "vector")
        copy_y(2, "vector")
        for g in range(2):
            quantise_w(0, g)
        quantise_y(1)
        quantise_y(2)

        product1(3)
        product1(4)
        for i in FIRST:
            product2(i, 0)
        product1(5)

        steps(3)
        for g in range(2):
            quantise_w(1, g)
        steps(4)
        step(5, 0)
        quantise_x(6)
        quantise_x(7)
        step(5, 1)
        for i in FIRST:
            copy_out(i, 0, "scalar")

        for i in FIRST:
            product2(i, 1)
        product1(6)
        product1(7)

        for i in FIRST:
            copy_out(i, 1, "scalar")
            store(i)
        steps(6)
        steps(7)

        for i in REST:
            transpose_y(i)
        copy_y(3, "scalar")
        copy_y(4, "vector")
        quantise_y(3)
        quantise_y(4)
        copy_y(5, "scalar")
        copy_y(6, "vector")
        quantise_y(5)
        copy_y(7, "scalar")

        finish(3)
        quantise_y(6)
        quantise_y(7)
        for i in (4, 5, 6, 7):
            finish(i)
